import numpy as np
import ml_dtypes


def mxq(x, axis, fmt="e4m3"):
    dtype, down = {"e4m3": (ml_dtypes.float8_e4m3fn, 7), "e5m2": (ml_dtypes.float8_e5m2, 14)}[fmt]
    v = np.moveaxis(np.asarray(x, np.float32).astype(ml_dtypes.bfloat16).astype(np.float64), axis, -1)
    blocks = v.reshape(v.shape[:-1] + (-1, 32))
    amax = np.abs(blocks).max(-1, keepdims=True)
    byte = np.maximum(np.where(amax > 0, np.frexp(amax)[1] - 1 + 127, 0) - down, 1)
    scale = np.exp2(byte - 127.0)
    codes = (blocks / scale).astype(np.float32).astype(dtype).astype(np.float64)
    return np.moveaxis((codes * scale).reshape(v.shape), -1, axis)


WIDE = False


def mx_kscale(k):
    if not WIDE:
        return np.ones(k)
    levels = np.array([10, -10, 5, -5, 0])
    a = np.random.permutation(np.resize(levels, k // 512 * 4)).reshape(k // 512, 4)
    idx = np.arange(k)
    return np.exp2(a[idx // 512, idx % 128 // 32])


BF16 = ml_dtypes.bfloat16


def bf(x):
    return np.asarray(x, np.float32).astype(BF16)


def f64(x):
    return np.asarray(x).astype(np.float64)


E2M1 = np.array([0.0, 0.5, 1.0, 1.5, 2.0, 3.0, 4.0, 6.0, -0.0, -0.5, -1.0, -1.5, -2.0, -3.0, -4.0, -6.0])


def pack_weight(w, fmt):
    k, n = w.shape
    w = f64(bf(w)).reshape(k // 32, 32, n)
    amax = np.abs(w).max(1)
    if fmt == "e4m3":
        byte = np.frexp(amax)[1] - 1 + 127 - 7
    else:
        mant, ex = np.frexp(amax / 6.0)
        byte = np.where(mant > 0.5, ex, ex - 1) + 127
    byte = np.clip(np.where(amax > 0, byte, 1), 1, 254)
    scaled = (w * np.exp2(127.0 - byte)[:, None, :]).reshape(k, n).astype(np.float32)
    by_word = np.ascontiguousarray(scaled.reshape(k // 512, 128, 4, n).transpose(0, 1, 3, 2))
    if fmt == "e4m3":
        words = by_word.astype(ml_dtypes.float8_e4m3fn).view(np.uint8)
    else:
        c = by_word.astype(ml_dtypes.float4_e2m1fn).view(np.uint8) & 0xF
        words = c[..., 0::2] | (c[..., 1::2] << 4)
    return np.ascontiguousarray(words), np.ascontiguousarray(byte.astype(np.uint8).reshape(k // 512, 16, n))


def unpack_weight(words, scales, fmt):
    g, p, n, _ = words.shape
    if fmt == "e4m3":
        vals = np.ascontiguousarray(words).view(ml_dtypes.float8_e4m3fn).astype(np.float64)
    else:
        nib = np.empty((g, p, n, 4), np.uint8)
        nib[..., 0::2] = words & 0xF
        nib[..., 1::2] = words >> 4
        vals = E2M1[nib]
    vals = vals * np.repeat(np.exp2(scales.astype(np.float64) - 127.0), 8, axis=1)[..., None]
    return vals.transpose(0, 1, 3, 2).reshape(g * 512, n)


N, IN_DIM, HID, NUM_CLASSES, AVG_DEG = 2048, 512, 512, 512, 32


def sigmoid(v):
    return 1.0 / (1.0 + np.exp(-v))


def setup_inputs():
    t = mx_kscale(HID)
    edges = np.random.uniform(size=(N, N)) < AVG_DEG / N
    A = bf(edges * (0.5 + np.random.uniform(size=(N, N))))
    deg_inv_sqrt = bf(1.0 / np.sqrt(1.0 + AVG_DEG * (0.75 + 0.5 * np.random.uniform(size=N))))
    h1 = bf(np.maximum(np.random.standard_normal((N, HID)) * 2.0 / np.sqrt(AVG_DEG), 0.0) * t)
    W2_words, W2_scales = pack_weight(np.random.standard_normal((HID, NUM_CLASSES)) * 4.0 / np.sqrt(HID) / t[:, None], "e4m3")
    b2 = bf(np.random.standard_normal(NUM_CLASSES) * 0.1)
    x = bf(np.random.standard_normal((N, NUM_CLASSES)) * 0.5)
    sigmoid_param = bf(4.0 + 0.4 * np.random.standard_normal(1))
    return {"A": A,
            "deg_inv_sqrt": deg_inv_sqrt,
            "h1": h1,
            "W2_words": W2_words,
            "W2_scales": W2_scales,
            "b2": b2,
            "x": x,
            "sigmoid_param": sigmoid_param}


def reference(A, deg_inv_sqrt, h1, W2_words, W2_scales, b2, x, sigmoid_param):
    dis = f64(deg_inv_sqrt)[:, None]
    g = mxq(f64(h1), 1, "e4m3") @ unpack_weight(W2_words, W2_scales, "e4m3")
    m = dis * g
    agg = mxq(f64(A), 0, "e4m3").T @ mxq(m, 0, "e4m3")
    h = dis * agg + dis ** 2 * g + f64(b2)
    return sigmoid(f64(sigmoid_param) * (h + f64(x)))

@@ -1,0 +1,198 @@
+from contextlib import ExitStack
+
+import concourse.mybir as mybir
+from concourse.masks import make_identity
+
+NODES = 2048
+HID = 512
+CLASSES = 512
+FLOPS = 2 * NODES * HID * CLASSES + 2 * NODES * NODES * CLASSES
+
+P = 128
+PACK = 4
+K_PASS = P * PACK
+GROUPS = NODES // K_PASS
+
+BF16 = mybir.dt.bfloat16
+F32 = mybir.dt.float32
+I32 = mybir.dt.int32
+U32 = mybir.dt.uint32
+U8 = mybir.dt.uint8
+FP8X4 = mybir.dt.float8_e4m3fn_x4
+ACT = mybir.ActivationFunctionType
+ALU = mybir.AluOpType
+
+
+def tile_gcnnodeclassifiernetwork_pb_kernel(
+    tc, A, deg_inv_sqrt, h1, W2_words, W2_scales, b2, x, sigmoid_param, out
+):
+    nc = tc.nc
+    by_group = "(g p j) f -> g p j f"
+    h1_dram = h1.rearrange(by_group, p=P, j=PACK)
+    x_dram = x.rearrange(by_group, p=P, j=PACK)
+    out_dram = out.rearrange(by_group, p=P, j=PACK)
+    a_dram = A.rearrange(by_group, p=P, j=PACK)
+
+    with ExitStack() as ctx:
+        keep = ctx.enter_context(tc.tile_pool(name="keep", bufs=1))
+        grouped_pool = ctx.enter_context(tc.tile_pool(name="grouped", bufs=5))
+        a_mx_pool = ctx.enter_context(tc.tile_pool(name="a_mx", bufs=2 * GROUPS))
+        sum_pool = ctx.enter_context(tc.tile_pool(name="sums", bufs=3))
+        result_pool = ctx.enter_context(tc.tile_pool(name="results", bufs=2))
+        psum_t = ctx.enter_context(tc.psum_pool(name="psum_t", bufs=2))
+        psum_acc = ctx.enter_context(tc.psum_pool(name="psum_acc", bufs=6))
+
+        w2_plane = keep.tile([P, CLASSES], U8, align_bytes=64)
+        nc.vector.memset(w2_plane[:].bitcast(I32), 0)
+        for quadrant in range(4):
+            nc.sync.dma_start(
+                out=w2_plane[32 * quadrant : 32 * quadrant + 4, :].bitcast(I32),
+                in_=W2_scales[0, 4 * quadrant : 4 * quadrant + 4, :].bitcast(I32),
+            )
+        w2_codes = keep.tile([P, PACK * CLASSES], U8, align_bytes=64)
+        nc.sync.dma_start(
+            out=w2_codes[:].bitcast(I32), in_=W2_words[0].rearrange("p n t -> p (n t)").bitcast(I32)
+        )
+
+        h1_sb = []
+        for g in range(GROUPS):
+            h1_sb.append(keep.tile([P, PACK, HID], BF16, name="h1_sb%d" % g))
+            nc.sync.dma_start(out=h1_sb[g][:], in_=h1_dram[g])
+
+        a_raw = [[None] * GROUPS for r in range(GROUPS)]
+        x_sb = []
+        for r in range(GROUPS):
+            x_sb.append(keep.tile([P, PACK, CLASSES], BF16, name="x_sb%d" % r))
+            nc.sync.dma_start(out=x_sb[r][:], in_=x_dram[r])
+            for c in range(GROUPS):
+                a_raw[r][c] = keep.tile([P, PACK, K_PASS], BF16, name="a_raw%d_%d" % (r, c))
+                nc.sync.dma_start(out=a_raw[r][c][:], in_=a_dram[c][:, :, K_PASS * r : K_PASS * (r + 1)])
+
+        d_bf16 = keep.tile([P, GROUPS, PACK], BF16)
+        nc.scalar.dma_start(out=d_bf16[:], in_=deg_inv_sqrt.rearrange("(g p j) -> p g j", p=P, j=PACK))
+        slope_bf16 = keep.tile([P, 1], BF16)
+        nc.scalar.dma_start(out=slope_bf16[:], in_=sigmoid_param.partition_broadcast(P))
+        b2_row = keep.tile([P, CLASSES], BF16)
+        nc.vector.memset(b2_row[:], 0.0)
+        nc.scalar.dma_start(out=b2_row[0:1, :], in_=b2.unsqueeze(0))
+
+        warm = keep.tile([P, 1], F32)
+        nc.vector.memset(warm[:], 0.0)
+        nc.scalar.activation(out=warm[:], in_=warm[:], func=ACT.Sigmoid)
+
+        ident = keep.tile([P, P], F32)
+        make_identity(nc, ident[:])
+        ones = keep.tile([P, P], BF16)
+        nc.vector.memset(ones[:], 1.0)
+
+        d = keep.tile([P, GROUPS * PACK], F32)
+        nc.vector.tensor_copy(out=d[:], in_=d_bf16[:].rearrange("p g j -> p (g j)"))
+        slope = keep.tile([P, 1], F32)
+        nc.vector.tensor_copy(out=slope[:], in_=slope_bf16[:])
+
+        b2_ps = psum_acc.tile([P, CLASSES], F32, tag="acc")
+        nc.tensor.matmul(b2_ps[:], lhsT=ones[:], rhs=b2_row[:], start=True, stop=True)
+        b2_all = keep.tile([P, CLASSES], F32)
+        nc.vector.tensor_copy(out=b2_all[:], in_=b2_ps[:])
+
+        m32 = []
+        m_codes = []
+        m_plane = []
+        for g in range(GROUPS):
+            h1t = grouped_pool.tile([P, PACK * K_PASS], BF16, align_bytes=64, tag="grouped")
+            h1t_words = h1t[:].bitcast(F32).rearrange("q (j n u) -> q j n u", j=PACK, u=2)
+            for half in range(2):
+                bank = psum_t.tile([P, 2, 2, P], F32)
+                for lane in range(2):
+                    words = h1_sb[g][:, 2 * half + lane, :].bitcast(F32)
+                    for u in range(2):
+                        nc.tensor.transpose(bank[:, lane, u, :], words[:, u : HID // 2 : 2], ident[:])
+                nc.scalar.copy(
+                    out=h1t_words[:, 2 * half : 2 * half + 2], in_=bank[:].rearrange("q j u n -> q j n u")
+                )
+            h1t_codes = keep.tile([P, K_PASS], U32, align_bytes=64, name="h1t_codes%d" % g)
+            h1t_plane = keep.tile([P, K_PASS], U8, align_bytes=64, name="h1t_plane%d" % g)
+            nc.vector.quantize_mx(out=h1t_codes[:].bitcast(FP8X4), scales=h1t_plane[:], in_=h1t[:])
+
+            m32.append(keep.tile([P, PACK, CLASSES], F32, name="m32_%d" % g))
+            for j in range(PACK):
+                lane_cols = slice(P * j, P * (j + 1))
+                g_ps = psum_acc.tile([P, CLASSES], F32, tag="acc")
+                nc.tensor.matmul_mx(
+                    out=g_ps[:],
+                    lhsT=h1t_codes[:, lane_cols].bitcast(FP8X4),
+                    lhsT_scale=h1t_plane[:, lane_cols],
+                    rhs=w2_codes[:].bitcast(FP8X4),
+                    rhs_scale=w2_plane[:],
+                    start=True,
+                    stop=True,
+                )
+                nc.scalar.activation(
+                    out=m32[g][:, j, :], in_=g_ps[:], func=ACT.Copy, scale=d[:, PACK * g + j : PACK * g + j + 1]
+                )
+
+            m_grouped = grouped_pool.tile([P, PACK * CLASSES], BF16, align_bytes=64, tag="grouped")
+            nc.vector.tensor_copy(
+                out=m_grouped[:].rearrange("p (n i j) -> p n j i", i=4, j=PACK),
+                in_=m32[g][:].rearrange("p j (n i) -> p n j i", i=4),
+            )
+            m_codes.append(keep.tile([P, CLASSES], U32, align_bytes=64, name="m_codes%d" % g))
+            m_plane.append(keep.tile([P, CLASSES], U8, align_bytes=64, name="m_plane%d" % g))
+            nc.vector.quantize_mx(out=m_codes[g][:].bitcast(FP8X4), scales=m_plane[g][:], in_=m_grouped[:])
+
+        for r in range(GROUPS):
+            for j in range(PACK):
+                nc.vector.scalar_tensor_tensor(
+                    out=m32[r][:, j, :],
+                    in0=m32[r][:, j, :],
+                    scalar=d[:, PACK * r + j : PACK * r + j + 1],
+                    in1=x_sb[r][:, j, :],
+                    op0=ALU.mult,
+                    op1=ALU.add,
+                )
+            nc.vector.tensor_tensor(
+                out=m32[r][:],
+                in0=m32[r][:],
+                in1=b2_all[:].unsqueeze(1).to_broadcast([P, PACK, CLASSES]),
+                op=ALU.add,
+            )
+
+            a_codes = []
+            a_plane = []
+            for c in range(GROUPS):
+                a_grouped = grouped_pool.tile([P, PACK * K_PASS], BF16, align_bytes=64, tag="grouped")
+                grouped_view = a_grouped[:].rearrange("p (j q t) -> p q t j", j=PACK, t=PACK)
+                raw_view = a_raw[r][c][:].rearrange("p t (q j) -> p q t j", j=PACK)
+                if c == GROUPS - 1:
+                    nc.vector.tensor_copy(out=grouped_view, in_=raw_view)
+                else:
+                    nc.scalar.copy(out=grouped_view, in_=raw_view)
+                a_codes.append(a_mx_pool.tile([P, K_PASS], U32, align_bytes=64, tag="a_codes", name="a_codes"))
+                a_plane.append(a_mx_pool.tile([P, K_PASS], U8, align_bytes=64, tag="a_plane", name="a_plane"))
+                nc.vector.quantize_mx(out=a_codes[c][:].bitcast(FP8X4), scales=a_plane[c][:], in_=a_grouped[:])
+
+            result = result_pool.tile([P, PACK, CLASSES], F32)
+            for j in range(PACK):
+                lane_cols = slice(P * j, P * (j + 1))
+                agg_ps = psum_acc.tile([P, CLASSES], F32, tag="acc")
+                for c in range(GROUPS):
+                    nc.tensor.matmul_mx(
+                        out=agg_ps[:],
+                        lhsT=a_codes[c][:, lane_cols].bitcast(FP8X4),
+                        lhsT_scale=a_plane[c][:, lane_cols],
+                        rhs=m_codes[c][:].bitcast(FP8X4),
+                        rhs_scale=m_plane[c][:],
+                        start=(c == 0),
+                        stop=(c == GROUPS - 1),
+                    )
+                total = sum_pool.tile([P, CLASSES], F32)
+                nc.vector.scalar_tensor_tensor(
+                    out=total[:],
+                    in0=agg_ps[:],
+                    scalar=d[:, PACK * r + j : PACK * r + j + 1],
+                    in1=m32[r][:, j, :],
+                    op0=ALU.mult,
+                    op1=ALU.add,
+                )
+                nc.scalar.activation(out=result[:, j, :], in_=total[:], func=ACT.Sigmoid, scale=slope[:, 0:1])
+            nc.sync.dma_start(out=out_dram[r], in_=result[:])

@@ -37,10 +37,30 @@ def tile_gcnnodeclassifiernetwork_pb_kernel(
         keep = ctx.enter_context(tc.tile_pool(name="keep", bufs=1))
         grouped_pool = ctx.enter_context(tc.tile_pool(name="grouped", bufs=5))
         a_mx_pool = ctx.enter_context(tc.tile_pool(name="a_mx", bufs=2 * GROUPS))
-        sum_pool = ctx.enter_context(tc.tile_pool(name="sums", bufs=3))
-        result_pool = ctx.enter_context(tc.tile_pool(name="results", bufs=2))
-        psum_t = ctx.enter_context(tc.psum_pool(name="psum_t", bufs=2))
-        psum_acc = ctx.enter_context(tc.psum_pool(name="psum_acc", bufs=6))
+        total_pool = ctx.enter_context(tc.tile_pool(name="totals", bufs=3))
+        result_pool = ctx.enter_context(tc.tile_pool(name="results", bufs=4))
+        psum_mx = ctx.enter_context(tc.psum_pool(name="psum_mx", bufs=4))
+        psum_plain = ctx.enter_context(tc.psum_pool(name="psum_plain", bufs=4))
+        ctx.enter_context(tc.manual_schedule())
+
+        h1_sb = [keep.tile([P, PACK, HID], BF16, name="h1_sb%d" % g) for g in range(GROUPS)]
+        x_sb = [keep.tile([P, PACK, CLASSES], BF16, name="x_sb%d" % g) for g in range(GROUPS)]
+        a_raw = {}
+        for r in range(GROUPS):
+            for c in range(GROUPS):
+                a_raw[r, c] = keep.tile([P, PACK, K_PASS], BF16, name="a_raw%d_%d" % (r, c))
+        h1t_codes = [keep.tile([P, K_PASS], U32, align_bytes=64, name="h1t_codes%d" % g) for g in range(GROUPS)]
+        h1t_plane = [keep.tile([P, K_PASS], U8, align_bytes=64, name="h1t_plane%d" % g) for g in range(GROUPS)]
+        m_codes = [keep.tile([P, CLASSES], U32, align_bytes=64, name="m_codes%d" % g) for g in range(GROUPS)]
+        m_plane = [keep.tile([P, CLASSES], U8, align_bytes=64, name="m_plane%d" % g) for g in range(GROUPS)]
+        own = [keep.tile([P, PACK, CLASSES], F32, name="own%d" % g) for g in range(GROUPS)]
+        grouped = {}
+        a_codes = {}
+        a_plane = {}
+        agg_ps = {}
+
+        def load_a(r, c):
+            nc.sync.dma_start(out=a_raw[r, c][:], in_=a_dram[c][:, :, K_PASS * r : K_PASS * (r + 1)])
 
         w2_plane = keep.tile([P, CLASSES], U8, align_bytes=64)
         nc.vector.memset(w2_plane[:].bitcast(I32), 0)
@@ -53,20 +73,16 @@ def tile_gcnnodeclassifiernetwork_pb_kernel(
         nc.sync.dma_start(
             out=w2_codes[:].bitcast(I32), in_=W2_words[0].rearrange("p n t -> p (n t)").bitcast(I32)
         )
-
-        h1_sb = []
-        for g in range(GROUPS):
-            h1_sb.append(keep.tile([P, PACK, HID], BF16, name="h1_sb%d" % g))
-            nc.sync.dma_start(out=h1_sb[g][:], in_=h1_dram[g])
-
-        a_raw = [[None] * GROUPS for r in range(GROUPS)]
-        x_sb = []
-        for r in range(GROUPS):
-            x_sb.append(keep.tile([P, PACK, CLASSES], BF16, name="x_sb%d" % r))
-            nc.sync.dma_start(out=x_sb[r][:], in_=x_dram[r])
+        for first in (0, 2):
+            for g in (first, first + 1):
+                nc.sync.dma_start(out=h1_sb[g][:], in_=h1_dram[g])
+            for c in (first, first + 1):
+                load_a(0, c)
+        nc.sync.dma_start(out=x_sb[0][:], in_=x_dram[0])
+        for r in range(1, GROUPS):
             for c in range(GROUPS):
-                a_raw[r][c] = keep.tile([P, PACK, K_PASS], BF16, name="a_raw%d_%d" % (r, c))
-                nc.sync.dma_start(out=a_raw[r][c][:], in_=a_dram[c][:, :, K_PASS * r : K_PASS * (r + 1)])
+                load_a(r, c)
+            nc.sync.dma_start(out=x_sb[r][:], in_=x_dram[r])
 
         d_bf16 = keep.tile([P, GROUPS, PACK], BF16)
         nc.scalar.dma_start(out=d_bf16[:], in_=deg_inv_sqrt.rearrange("(g p j) -> p g j", p=P, j=PACK))
@@ -80,8 +96,10 @@ def tile_gcnnodeclassifiernetwork_pb_kernel(
         nc.vector.memset(warm[:], 0.0)
         nc.scalar.activation(out=warm[:], in_=warm[:], func=ACT.Sigmoid)
 
-        ident = keep.tile([P, P], F32)
-        make_identity(nc, ident[:])
+        ident_f32 = keep.tile([P, P], F32)
+        make_identity(nc, ident_f32[:])
+        ident_bf16 = keep.tile([P, P], BF16)
+        make_identity(nc, ident_bf16[:])
         ones = keep.tile([P, P], BF16)
         nc.vector.memset(ones[:], 1.0)
 
@@ -90,109 +108,135 @@ def tile_gcnnodeclassifiernetwork_pb_kernel(
         slope = keep.tile([P, 1], F32)
         nc.vector.tensor_copy(out=slope[:], in_=slope_bf16[:])
 
-        b2_ps = psum_acc.tile([P, CLASSES], F32, tag="acc")
-        nc.tensor.matmul(b2_ps[:], lhsT=ones[:], rhs=b2_row[:], start=True, stop=True)
-        b2_all = keep.tile([P, CLASSES], F32)
-        nc.vector.tensor_copy(out=b2_all[:], in_=b2_ps[:])
+        def d_of(g, j):
+            return d[:, PACK * g + j : PACK * g + j + 1]
 
-        m32 = []
-        m_codes = []
-        m_plane = []
-        for g in range(GROUPS):
+        def transpose_h1(g):
             h1t = grouped_pool.tile([P, PACK * K_PASS], BF16, align_bytes=64, tag="grouped")
+            grouped["h1", g] = h1t
             h1t_words = h1t[:].bitcast(F32).rearrange("q (j n u) -> q j n u", j=PACK, u=2)
             for half in range(2):
-                bank = psum_t.tile([P, 2, 2, P], F32)
+                bank = psum_plain.tile([P, 2, 2, P], F32, tag="plain")
                 for lane in range(2):
                     words = h1_sb[g][:, 2 * half + lane, :].bitcast(F32)
                     for u in range(2):
-                        nc.tensor.transpose(bank[:, lane, u, :], words[:, u : HID // 2 : 2], ident[:])
+                        nc.tensor.transpose(bank[:, lane, u, :], words[:, u : HID // 2 : 2], ident_f32[:])
                 nc.scalar.copy(
                     out=h1t_words[:, 2 * half : 2 * half + 2], in_=bank[:].rearrange("q j u n -> q j n u")
                 )
-            h1t_codes = keep.tile([P, K_PASS], U32, align_bytes=64, name="h1t_codes%d" % g)
-            h1t_plane = keep.tile([P, K_PASS], U8, align_bytes=64, name="h1t_plane%d" % g)
-            nc.vector.quantize_mx(out=h1t_codes[:].bitcast(FP8X4), scales=h1t_plane[:], in_=h1t[:])
 
-            m32.append(keep.tile([P, PACK, CLASSES], F32, name="m32_%d" % g))
+        def quantise_h1(g):
+            nc.vector.quantize_mx(
+                out=h1t_codes[g][:].bitcast(FP8X4), scales=h1t_plane[g][:], in_=grouped["h1", g][:]
+            )
+
+        def first_matmul(g):
             for j in range(PACK):
                 lane_cols = slice(P * j, P * (j + 1))
-                g_ps = psum_acc.tile([P, CLASSES], F32, tag="acc")
+                g_ps = psum_mx.tile([P, CLASSES], F32, tag="mx")
                 nc.tensor.matmul_mx(
                     out=g_ps[:],
-                    lhsT=h1t_codes[:, lane_cols].bitcast(FP8X4),
-                    lhsT_scale=h1t_plane[:, lane_cols],
+                    lhsT=h1t_codes[g][:, lane_cols].bitcast(FP8X4),
+                    lhsT_scale=h1t_plane[g][:, lane_cols],
                     rhs=w2_codes[:].bitcast(FP8X4),
                     rhs_scale=w2_plane[:],
                     start=True,
                     stop=True,
                 )
-                nc.scalar.activation(
-                    out=m32[g][:, j, :], in_=g_ps[:], func=ACT.Copy, scale=d[:, PACK * g + j : PACK * g + j + 1]
-                )
+                nc.scalar.activation(out=own[g][:, j, :], in_=g_ps[:], func=ACT.Copy, scale=d_of(g, j))
 
+        def regroup_m(g):
             m_grouped = grouped_pool.tile([P, PACK * CLASSES], BF16, align_bytes=64, tag="grouped")
+            grouped["m", g] = m_grouped
             nc.vector.tensor_copy(
                 out=m_grouped[:].rearrange("p (n i j) -> p n j i", i=4, j=PACK),
-                in_=m32[g][:].rearrange("p j (n i) -> p n j i", i=4),
+                in_=own[g][:].rearrange("p j (n i) -> p n j i", i=4),
             )
-            m_codes.append(keep.tile([P, CLASSES], U32, align_bytes=64, name="m_codes%d" % g))
-            m_plane.append(keep.tile([P, CLASSES], U8, align_bytes=64, name="m_plane%d" % g))
-            nc.vector.quantize_mx(out=m_codes[g][:].bitcast(FP8X4), scales=m_plane[g][:], in_=m_grouped[:])
+
+        def quantise_m(g):
+            nc.vector.quantize_mx(out=m_codes[g][:].bitcast(FP8X4), scales=m_plane[g][:], in_=grouped["m", g][:])
+
+        def regroup_a(r, c, copy):
+            a_grouped = grouped_pool.tile([P, PACK * K_PASS], BF16, align_bytes=64, tag="grouped")
+            grouped["a", r, c] = a_grouped
+            copy(
+                out=a_grouped[:].rearrange("p (j q t) -> p q t j", j=PACK, t=PACK),
+                in_=a_raw[r, c][:].rearrange("p t (q j) -> p q t j", j=PACK),
+            )
+
+        def quantise_a(r, c):
+            a_codes[r, c] = a_mx_pool.tile([P, K_PASS], U32, align_bytes=64, tag="a_codes", name="a_codes")
+            a_plane[r, c] = a_mx_pool.tile([P, K_PASS], U8, align_bytes=64, tag="a_plane", name="a_plane")
+            nc.vector.quantize_mx(
+                out=a_codes[r, c][:].bitcast(FP8X4), scales=a_plane[r, c][:], in_=grouped["a", r, c][:]
+            )
+
+        def add_skip_and_bias(r):
+            for j in range(PACK):
+                skip_ps = psum_plain.tile([P, CLASSES], F32, tag="plain")
+                nc.tensor.matmul(skip_ps[:], lhsT=ident_bf16[:], rhs=x_sb[r][:, j, :], start=True, stop=False)
+                nc.tensor.matmul(skip_ps[:], lhsT=ones[:], rhs=b2_row[:], start=False, stop=True)
+                nc.vector.scalar_tensor_tensor(
+                    out=own[r][:, j, :],
+                    in0=own[r][:, j, :],
+                    scalar=d_of(r, j),
+                    in1=skip_ps[:],
+                    op0=ALU.mult,
+                    op1=ALU.add,
+                )
+
+        def second_matmul(r, j):
+            lane_cols = slice(P * j, P * (j + 1))
+            agg_ps[r, j] = psum_mx.tile([P, CLASSES], F32, tag="mx", name="agg_ps")
+            for c in range(GROUPS):
+                nc.tensor.matmul_mx(
+                    out=agg_ps[r, j][:],
+                    lhsT=a_codes[r, c][:, lane_cols].bitcast(FP8X4),
+                    lhsT_scale=a_plane[r, c][:, lane_cols],
+                    rhs=m_codes[c][:].bitcast(FP8X4),
+                    rhs_scale=m_plane[c][:],
+                    start=(c == 0),
+                    stop=(c == GROUPS - 1),
+                )
+
+        def finish(r, j):
+            total = total_pool.tile([P, CLASSES], F32)
+            nc.vector.scalar_tensor_tensor(
+                out=total[:], in0=agg_ps[r, j][:], scalar=d_of(r, j), in1=own[r][:, j, :], op0=ALU.mult, op1=ALU.add
+            )
+            result = result_pool.tile([P, CLASSES], F32)
+            nc.scalar.activation(out=result[:], in_=total[:], func=ACT.Sigmoid, scale=slope[:, 0:1])
+            nc.sync.dma_start(out=out_dram[r][:, j, :], in_=result[:])
+
+        VECTOR_CHUNKS = GROUPS - 1
+        transpose_h1(0)
+        transpose_h1(1)
+        for k in range(GROUPS + 2):
+            if 1 <= k <= VECTOR_CHUNKS:
+                regroup_a(0, k - 1, nc.vector.tensor_copy)
+            if k >= 2:
+                regroup_m(k - 2)
+            if k < GROUPS:
+                quantise_h1(k)
+                first_matmul(k)
+                if k + 2 < GROUPS:
+                    transpose_h1(k + 2)
+            if 1 <= k <= VECTOR_CHUNKS:
+                quantise_a(0, k - 1)
+            if k >= 2:
+                quantise_m(k - 2)
+        regroup_a(0, GROUPS - 1, nc.scalar.copy)
+        add_skip_and_bias(0)
+        quantise_a(0, GROUPS - 1)
 
         for r in range(GROUPS):
+            if r + 1 < GROUPS:
+                for c in range(GROUPS - 1):
+                    regroup_a(r + 1, c, nc.scalar.copy)
+                add_skip_and_bias(r + 1)
+                regroup_a(r + 1, GROUPS - 1, nc.vector.tensor_copy)
             for j in range(PACK):
-                nc.vector.scalar_tensor_tensor(
-                    out=m32[r][:, j, :],
-                    in0=m32[r][:, j, :],
-                    scalar=d[:, PACK * r + j : PACK * r + j + 1],
-                    in1=x_sb[r][:, j, :],
-                    op0=ALU.mult,
-                    op1=ALU.add,
-                )
-            nc.vector.tensor_tensor(
-                out=m32[r][:],
-                in0=m32[r][:],
-                in1=b2_all[:].unsqueeze(1).to_broadcast([P, PACK, CLASSES]),
-                op=ALU.add,
-            )
-
-            a_codes = []
-            a_plane = []
-            for c in range(GROUPS):
-                a_grouped = grouped_pool.tile([P, PACK * K_PASS], BF16, align_bytes=64, tag="grouped")
-                grouped_view = a_grouped[:].rearrange("p (j q t) -> p q t j", j=PACK, t=PACK)
-                raw_view = a_raw[r][c][:].rearrange("p t (q j) -> p q t j", j=PACK)
-                if c == GROUPS - 1:
-                    nc.vector.tensor_copy(out=grouped_view, in_=raw_view)
-                else:
-                    nc.scalar.copy(out=grouped_view, in_=raw_view)
-                a_codes.append(a_mx_pool.tile([P, K_PASS], U32, align_bytes=64, tag="a_codes", name="a_codes"))
-                a_plane.append(a_mx_pool.tile([P, K_PASS], U8, align_bytes=64, tag="a_plane", name="a_plane"))
-                nc.vector.quantize_mx(out=a_codes[c][:].bitcast(FP8X4), scales=a_plane[c][:], in_=a_grouped[:])
-
-            result = result_pool.tile([P, PACK, CLASSES], F32)
-            for j in range(PACK):
-                lane_cols = slice(P * j, P * (j + 1))
-                agg_ps = psum_acc.tile([P, CLASSES], F32, tag="acc")
-                for c in range(GROUPS):
-                    nc.tensor.matmul_mx(
-                        out=agg_ps[:],
-                        lhsT=a_codes[c][:, lane_cols].bitcast(FP8X4),
-                        lhsT_scale=a_plane[c][:, lane_cols],
-                        rhs=m_codes[c][:].bitcast(FP8X4),
-                        rhs_scale=m_plane[c][:],
-                        start=(c == 0),
-                        stop=(c == GROUPS - 1),
-                    )
-                total = sum_pool.tile([P, CLASSES], F32)
-                nc.vector.scalar_tensor_tensor(
-                    out=total[:],
-                    in0=agg_ps[:],
-                    scalar=d[:, PACK * r + j : PACK * r + j + 1],
-                    in1=m32[r][:, j, :],
-                    op0=ALU.mult,
-                    op1=ALU.add,
-                )
-                nc.scalar.activation(out=result[:, j, :], in_=total[:], func=ACT.Sigmoid, scale=slope[:, 0:1])
-            nc.sync.dma_start(out=out_dram[r], in_=result[:])
+                second_matmul(r, j)
+                finish(r, j)
+                if r + 1 < GROUPS:
+                    quantise_a(r + 1, j)

@@ -12,6 +12,7 @@ P = 128
 PACK = 4
 K_PASS = P * PACK
 GROUPS = NODES // K_PASS
+LAST = GROUPS - 1
 
 BF16 = mybir.dt.bfloat16
 F32 = mybir.dt.float32
@@ -35,10 +36,10 @@ def tile_gcnnodeclassifiernetwork_pb_kernel(
 
     with ExitStack() as ctx:
         keep = ctx.enter_context(tc.tile_pool(name="keep", bufs=1))
-        grouped_pool = ctx.enter_context(tc.tile_pool(name="grouped", bufs=5))
+        grouped_pool = ctx.enter_context(tc.tile_pool(name="grouped", bufs=6))
         a_mx_pool = ctx.enter_context(tc.tile_pool(name="a_mx", bufs=2 * GROUPS))
-        total_pool = ctx.enter_context(tc.tile_pool(name="totals", bufs=3))
-        result_pool = ctx.enter_context(tc.tile_pool(name="results", bufs=4))
+        total_pool = ctx.enter_context(tc.tile_pool(name="totals", bufs=PACK))
+        result_pool = ctx.enter_context(tc.tile_pool(name="results", bufs=2 * PACK))
         psum_mx = ctx.enter_context(tc.psum_pool(name="psum_mx", bufs=4))
         psum_plain = ctx.enter_context(tc.psum_pool(name="psum_plain", bufs=4))
         ctx.enter_context(tc.manual_schedule())
@@ -62,6 +63,7 @@ def tile_gcnnodeclassifiernetwork_pb_kernel(
         def load_a(r, c):
             nc.sync.dma_start(out=a_raw[r, c][:], in_=a_dram[c][:, :, K_PASS * r : K_PASS * (r + 1)])
 
+        nc.sync.dma_start(out=h1_sb[0][:], in_=h1_dram[0])
         w2_plane = keep.tile([P, CLASSES], U8, align_bytes=64)
         nc.vector.memset(w2_plane[:].bitcast(I32), 0)
         for quadrant in range(4):
@@ -73,11 +75,13 @@ def tile_gcnnodeclassifiernetwork_pb_kernel(
         nc.sync.dma_start(
             out=w2_codes[:].bitcast(I32), in_=W2_words[0].rearrange("p n t -> p (n t)").bitcast(I32)
         )
-        for first in (0, 2):
-            for g in (first, first + 1):
-                nc.sync.dma_start(out=h1_sb[g][:], in_=h1_dram[g])
-            for c in (first, first + 1):
-                load_a(0, c)
+        nc.sync.dma_start(out=h1_sb[1][:], in_=h1_dram[1])
+        load_a(0, 0)
+        load_a(0, 1)
+        nc.sync.dma_start(out=h1_sb[2][:], in_=h1_dram[2])
+        nc.sync.dma_start(out=h1_sb[3][:], in_=h1_dram[3])
+        load_a(0, 2)
+        load_a(0, 3)
         nc.sync.dma_start(out=x_sb[0][:], in_=x_dram[0])
         for r in range(1, GROUPS):
             for c in range(GROUPS):
@@ -185,19 +189,20 @@ def tile_gcnnodeclassifiernetwork_pb_kernel(
                     op1=ALU.add,
                 )
 
-        def second_matmul(r, j):
+        def second_matmul_pass(r, j, c):
+            if c == 0:
+                bank_pool, bank_tag = (psum_plain, "plain") if r == LAST else (psum_mx, "mx")
+                agg_ps[r, j] = bank_pool.tile([P, CLASSES], F32, tag=bank_tag, name="agg_ps")
             lane_cols = slice(P * j, P * (j + 1))
-            agg_ps[r, j] = psum_mx.tile([P, CLASSES], F32, tag="mx", name="agg_ps")
-            for c in range(GROUPS):
-                nc.tensor.matmul_mx(
-                    out=agg_ps[r, j][:],
-                    lhsT=a_codes[r, c][:, lane_cols].bitcast(FP8X4),
-                    lhsT_scale=a_plane[r, c][:, lane_cols],
-                    rhs=m_codes[c][:].bitcast(FP8X4),
-                    rhs_scale=m_plane[c][:],
-                    start=(c == 0),
-                    stop=(c == GROUPS - 1),
-                )
+            nc.tensor.matmul_mx(
+                out=agg_ps[r, j][:],
+                lhsT=a_codes[r, c][:, lane_cols].bitcast(FP8X4),
+                lhsT_scale=a_plane[r, c][:, lane_cols],
+                rhs=m_codes[c][:].bitcast(FP8X4),
+                rhs_scale=m_plane[c][:],
+                start=(c == 0),
+                stop=(c == LAST),
+            )
 
         def finish(r, j):
             total = total_pool.tile([P, CLASSES], F32)
@@ -208,7 +213,7 @@ def tile_gcnnodeclassifiernetwork_pb_kernel(
             nc.scalar.activation(out=result[:], in_=total[:], func=ACT.Sigmoid, scale=slope[:, 0:1])
             nc.sync.dma_start(out=out_dram[r][:, j, :], in_=result[:])
 
-        VECTOR_CHUNKS = GROUPS - 1
+        VECTOR_CHUNKS = LAST
         transpose_h1(0)
         transpose_h1(1)
         for k in range(GROUPS + 2):
@@ -225,18 +230,28 @@ def tile_gcnnodeclassifiernetwork_pb_kernel(
                 quantise_a(0, k - 1)
             if k >= 2:
                 quantise_m(k - 2)
-        regroup_a(0, GROUPS - 1, nc.scalar.copy)
+        regroup_a(0, LAST, nc.scalar.copy)
+        regroup_a(1, 0, nc.scalar.copy)
         add_skip_and_bias(0)
-        quantise_a(0, GROUPS - 1)
+        quantise_a(0, LAST)
 
         for r in range(GROUPS):
             if r + 1 < GROUPS:
-                for c in range(GROUPS - 1):
-                    regroup_a(r + 1, c, nc.scalar.copy)
+                regroup_a(r + 1, 1, nc.scalar.copy)
+                regroup_a(r + 1, 2, nc.scalar.copy)
+            if r + 2 < GROUPS:
+                regroup_a(r + 2, 0, nc.scalar.copy)
+            if r + 1 < GROUPS:
                 add_skip_and_bias(r + 1)
-                regroup_a(r + 1, GROUPS - 1, nc.vector.tensor_copy)
+                regroup_a(r + 1, LAST, nc.vector.tensor_copy)
+            if r < LAST:
+                for j in range(PACK):
+                    for c in range(GROUPS):
+                        second_matmul_pass(r, j, c)
             for j in range(PACK):
-                second_matmul(r, j)
                 finish(r, j)
                 if r + 1 < GROUPS:
                     quantise_a(r + 1, j)
+                if r + 1 == LAST:
+                    for lane in range(PACK):
+                        second_matmul_pass(LAST, lane, j)

@@ -63,7 +63,9 @@ def tile_gcnnodeclassifiernetwork_pb_kernel(
         def load_a(r, c):
             nc.sync.dma_start(out=a_raw[r, c][:], in_=a_dram[c][:, :, K_PASS * r : K_PASS * (r + 1)])
 
-        nc.sync.dma_start(out=h1_sb[0][:], in_=h1_dram[0])
+        for half in range(2):
+            lanes = slice(2 * half, 2 * half + 2)
+            nc.sync.dma_start(out=h1_sb[0][:, lanes, :], in_=h1_dram[0][:, lanes, :])
         w2_plane = keep.tile([P, CLASSES], U8, align_bytes=64)
         nc.vector.memset(w2_plane[:].bitcast(I32), 0)
         for quadrant in range(4):
@@ -76,25 +78,24 @@ def tile_gcnnodeclassifiernetwork_pb_kernel(
             out=w2_codes[:].bitcast(I32), in_=W2_words[0].rearrange("p n t -> p (n t)").bitcast(I32)
         )
         nc.sync.dma_start(out=h1_sb[1][:], in_=h1_dram[1])
+        d_bf16 = keep.tile([P, GROUPS, PACK], BF16)
+        nc.sync.dma_start(out=d_bf16[:], in_=deg_inv_sqrt.rearrange("(g p j) -> p g j", p=P, j=PACK))
         load_a(0, 0)
         load_a(0, 1)
         nc.sync.dma_start(out=h1_sb[2][:], in_=h1_dram[2])
-        nc.sync.dma_start(out=h1_sb[3][:], in_=h1_dram[3])
         load_a(0, 2)
+        nc.sync.dma_start(out=h1_sb[3][:], in_=h1_dram[3])
         load_a(0, 3)
+        b2_row = keep.tile([P, CLASSES], BF16)
+        nc.vector.memset(b2_row[:], 0.0)
+        nc.sync.dma_start(out=b2_row[0:1, :], in_=b2.unsqueeze(0))
+        slope_bf16 = keep.tile([P, 1], BF16)
+        nc.sync.dma_start(out=slope_bf16[:], in_=sigmoid_param.partition_broadcast(P))
         nc.sync.dma_start(out=x_sb[0][:], in_=x_dram[0])
         for r in range(1, GROUPS):
             for c in range(GROUPS):
                 load_a(r, c)
             nc.sync.dma_start(out=x_sb[r][:], in_=x_dram[r])
-
-        d_bf16 = keep.tile([P, GROUPS, PACK], BF16)
-        nc.scalar.dma_start(out=d_bf16[:], in_=deg_inv_sqrt.rearrange("(g p j) -> p g j", p=P, j=PACK))
-        slope_bf16 = keep.tile([P, 1], BF16)
-        nc.scalar.dma_start(out=slope_bf16[:], in_=sigmoid_param.partition_broadcast(P))
-        b2_row = keep.tile([P, CLASSES], BF16)
-        nc.vector.memset(b2_row[:], 0.0)
-        nc.scalar.dma_start(out=b2_row[0:1, :], in_=b2.unsqueeze(0))
 
         warm = keep.tile([P, 1], F32)
         nc.vector.memset(warm[:], 0.0)
@@ -108,9 +109,7 @@ def tile_gcnnodeclassifiernetwork_pb_kernel(
         nc.vector.memset(ones[:], 1.0)
 
         d = keep.tile([P, GROUPS * PACK], F32)
-        nc.vector.tensor_copy(out=d[:], in_=d_bf16[:].rearrange("p g j -> p (g j)"))
         slope = keep.tile([P, 1], F32)
-        nc.vector.tensor_copy(out=slope[:], in_=slope_bf16[:])
 
         def d_of(g, j):
             return d[:, PACK * g + j : PACK * g + j + 1]
@@ -204,32 +203,42 @@ def tile_gcnnodeclassifiernetwork_pb_kernel(
                 stop=(c == LAST),
             )
 
-        def finish(r, j):
+        totals = {}
+
+        def finish_sum(r, j):
             total = total_pool.tile([P, CLASSES], F32)
+            totals[r, j] = total
             nc.vector.scalar_tensor_tensor(
                 out=total[:], in0=agg_ps[r, j][:], scalar=d_of(r, j), in1=own[r][:, j, :], op0=ALU.mult, op1=ALU.add
             )
+
+        def finish_sigmoid(r, j):
             result = result_pool.tile([P, CLASSES], F32)
-            nc.scalar.activation(out=result[:], in_=total[:], func=ACT.Sigmoid, scale=slope[:, 0:1])
+            nc.scalar.activation(out=result[:], in_=totals[r, j][:], func=ACT.Sigmoid, scale=slope[:, 0:1])
             nc.sync.dma_start(out=out_dram[r][:, j, :], in_=result[:])
 
         VECTOR_CHUNKS = LAST
         transpose_h1(0)
         transpose_h1(1)
-        for k in range(GROUPS + 2):
-            if 1 <= k <= VECTOR_CHUNKS:
-                regroup_a(0, k - 1, nc.vector.tensor_copy)
-            if k >= 2:
-                regroup_m(k - 2)
-            if k < GROUPS:
-                quantise_h1(k)
-                first_matmul(k)
-                if k + 2 < GROUPS:
-                    transpose_h1(k + 2)
-            if 1 <= k <= VECTOR_CHUNKS:
-                quantise_a(0, k - 1)
-            if k >= 2:
-                quantise_m(k - 2)
+        quantise_h1(0)
+        nc.gpsimd.tensor_copy(out=d[:], in_=d_bf16[:].rearrange("p g j -> p (g j)"))
+        first_matmul(0)
+        transpose_h1(2)
+        regroup_a(0, 0, nc.vector.tensor_copy)
+        quantise_h1(1)
+        first_matmul(1)
+        transpose_h1(3)
+        for k in range(GROUPS):
+            if k < VECTOR_CHUNKS:
+                quantise_a(0, k)
+            regroup_m(k)
+            if k + 2 < GROUPS:
+                quantise_h1(k + 2)
+                first_matmul(k + 2)
+            if k + 1 < VECTOR_CHUNKS:
+                regroup_a(0, k + 1, nc.vector.tensor_copy)
+            quantise_m(k)
+        nc.gpsimd.tensor_copy(out=slope[:], in_=slope_bf16[:])
         regroup_a(0, LAST, nc.scalar.copy)
         regroup_a(1, 0, nc.scalar.copy)
         add_skip_and_bias(0)
@@ -249,8 +258,11 @@ def tile_gcnnodeclassifiernetwork_pb_kernel(
                     for c in range(GROUPS):
                         second_matmul_pass(r, j, c)
             for j in range(PACK):
-                finish(r, j)
-                if r + 1 < GROUPS:
+                if (r + 1, j) == (LAST, LAST):
+                    quantise_a(r + 1, j)
+                finish_sum(r, j)
+                finish_sigmoid(r, j)
+                if r + 1 < GROUPS and (r + 1, j) != (LAST, LAST):
                     quantise_a(r + 1, j)
                 if r + 1 == LAST:
                     for lane in range(PACK):

@@ -167,15 +167,19 @@ def tile_gcnnodeclassifiernetwork_pb_kernel(
                 in_=a_raw[r, c][:].rearrange("p t (q j) -> p q t j", j=PACK),
             )
 
-        def quantise_a(r, c):
-            a_codes[r, c] = a_mx_pool.tile([P, K_PASS], U32, align_bytes=64, tag="a_codes", name="a_codes")
-            a_plane[r, c] = a_mx_pool.tile([P, K_PASS], U8, align_bytes=64, tag="a_plane", name="a_plane")
+        def quantise_a(r, c, lanes=slice(0, PACK)):
+            if (r, c) not in a_codes:
+                a_codes[r, c] = a_mx_pool.tile([P, K_PASS], U32, align_bytes=64, tag="a_codes", name="a_codes")
+                a_plane[r, c] = a_mx_pool.tile([P, K_PASS], U8, align_bytes=64, tag="a_plane", name="a_plane")
+            cols = slice(P * lanes.start, P * lanes.stop)
             nc.vector.quantize_mx(
-                out=a_codes[r, c][:].bitcast(FP8X4), scales=a_plane[r, c][:], in_=grouped["a", r, c][:]
+                out=a_codes[r, c][:, cols].bitcast(FP8X4),
+                scales=a_plane[r, c][:, cols],
+                in_=grouped["a", r, c][:, PACK * cols.start : PACK * cols.stop],
             )
 
-        def add_skip_and_bias(r):
-            for j in range(PACK):
+        def add_skip_and_bias(r, lanes=range(PACK)):
+            for j in lanes:
                 skip_ps = psum_plain.tile([P, CLASSES], F32, tag="plain")
                 nc.tensor.matmul(skip_ps[:], lhsT=ident_bf16[:], rhs=x_sb[r][:, j, :], start=True, stop=False)
                 nc.tensor.matmul(skip_ps[:], lhsT=ones[:], rhs=b2_row[:], start=False, stop=True)
@@ -204,18 +208,29 @@ def tile_gcnnodeclassifiernetwork_pb_kernel(
             )
 
         totals = {}
+        results = {}
+        EVERY = slice(0, CLASSES)
 
-        def finish_sum(r, j):
-            total = total_pool.tile([P, CLASSES], F32)
-            totals[r, j] = total
+        def finish_sum(r, j, classes=EVERY):
+            if (r, j) not in totals:
+                totals[r, j] = total_pool.tile([P, CLASSES], F32, name="total")
             nc.vector.scalar_tensor_tensor(
-                out=total[:], in0=agg_ps[r, j][:], scalar=d_of(r, j), in1=own[r][:, j, :], op0=ALU.mult, op1=ALU.add
+                out=totals[r, j][:, classes],
+                in0=agg_ps[r, j][:, classes],
+                scalar=d_of(r, j),
+                in1=own[r][:, j, classes],
+                op0=ALU.mult,
+                op1=ALU.add,
             )
 
-        def finish_sigmoid(r, j):
-            result = result_pool.tile([P, CLASSES], F32)
-            nc.scalar.activation(out=result[:], in_=totals[r, j][:], func=ACT.Sigmoid, scale=slope[:, 0:1])
-            nc.sync.dma_start(out=out_dram[r][:, j, :], in_=result[:])
+        def finish_sigmoid(r, j, classes=EVERY):
+            if (r, j) not in results:
+                results[r, j] = result_pool.tile([P, CLASSES], F32, name="result")
+            result = results[r, j]
+            nc.scalar.activation(
+                out=result[:, classes], in_=totals[r, j][:, classes], func=ACT.Sigmoid, scale=slope[:, 0:1]
+            )
+            nc.sync.dma_start(out=out_dram[r][:, j, classes], in_=result[:, classes])
 
         VECTOR_CHUNKS = LAST
         transpose_h1(0)
@@ -231,17 +246,21 @@ def tile_gcnnodeclassifiernetwork_pb_kernel(
         for k in range(GROUPS):
             if k < VECTOR_CHUNKS:
                 quantise_a(0, k)
+            if k == 0 and k + 1 < VECTOR_CHUNKS:
+                regroup_a(0, k + 1, nc.vector.tensor_copy)
             regroup_m(k)
             if k + 2 < GROUPS:
                 quantise_h1(k + 2)
                 first_matmul(k + 2)
-            if k + 1 < VECTOR_CHUNKS:
+            else:
+                add_skip_and_bias(0, [k - 2])
+            if k > 0 and k + 1 < VECTOR_CHUNKS:
                 regroup_a(0, k + 1, nc.vector.tensor_copy)
             quantise_m(k)
         nc.gpsimd.tensor_copy(out=slope[:], in_=slope_bf16[:])
         regroup_a(0, LAST, nc.scalar.copy)
         regroup_a(1, 0, nc.scalar.copy)
-        add_skip_and_bias(0)
+        add_skip_and_bias(0, [2, 3])
         quantise_a(0, LAST)
 
         for r in range(GROUPS):
@@ -259,11 +278,21 @@ def tile_gcnnodeclassifiernetwork_pb_kernel(
                         second_matmul_pass(r, j, c)
             for j in range(PACK):
                 if (r + 1, j) == (LAST, LAST):
-                    quantise_a(r + 1, j)
-                finish_sum(r, j)
-                finish_sigmoid(r, j)
-                if r + 1 < GROUPS and (r + 1, j) != (LAST, LAST):
+                    quantise_a(LAST, LAST, slice(0, 2))
+                halves = [slice(0, CLASSES // 2), slice(CLASSES // 2, CLASSES)] if (r, j) == (LAST, LAST) else [EVERY]
+                for classes in halves:
+                    finish_sum(r, j, classes)
+                    finish_sigmoid(r, j, classes)
+                if (r + 1, j) == (LAST, LAST):
+                    quantise_a(LAST, LAST, slice(2, PACK))
+                elif r + 1 < GROUPS:
                     quantise_a(r + 1, j)
                 if r + 1 == LAST:
-                    for lane in range(PACK):
-                        second_matmul_pass(LAST, lane, j)
+                    if j < 2:
+                        for lane in range(PACK):
+                            second_matmul_pass(LAST, lane, j)
+                    if j == LAST:
+                        for lanes in ((0, 1), (2, 3)):
+                            for c in (2, 3):
+                                for lane in lanes:
+                                    second_matmul_pass(LAST, lane, c)

@@ -28,7 +28,7 @@ def tile_gcnnodeclassifiernetwork_pb_kernel(
     tc, A, deg_inv_sqrt, h1, W2_words, W2_scales, b2, x, sigmoid_param, out
 ):
     nc = tc.nc
-    by_group = "(g p j) f -> g p j f"
+    by_group = "(g j p) f -> g p j f"
     h1_dram = h1.rearrange(by_group, p=P, j=PACK)
     x_dram = x.rearrange(by_group, p=P, j=PACK)
     out_dram = out.rearrange(by_group, p=P, j=PACK)
@@ -78,8 +78,9 @@ def tile_gcnnodeclassifiernetwork_pb_kernel(
             out=w2_codes[:].bitcast(I32), in_=W2_words[0].rearrange("p n t -> p (n t)").bitcast(I32)
         )
         nc.sync.dma_start(out=h1_sb[1][:], in_=h1_dram[1])
-        d_bf16 = keep.tile([P, GROUPS, PACK], BF16)
-        nc.sync.dma_start(out=d_bf16[:], in_=deg_inv_sqrt.rearrange("(g p j) -> p g j", p=P, j=PACK))
+        d_rows = keep.tile([P, P], BF16)
+        nc.vector.memset(d_rows[:], 0.0)
+        nc.sync.dma_start(out=d_rows[0 : GROUPS * PACK, :], in_=deg_inv_sqrt.rearrange("(r p) -> r p", p=P))
         load_a(0, 0)
         load_a(0, 1)
         nc.sync.dma_start(out=h1_sb[2][:], in_=h1_dram[2])
@@ -163,8 +164,8 @@ def tile_gcnnodeclassifiernetwork_pb_kernel(
             a_grouped = grouped_pool.tile([P, PACK * K_PASS], BF16, align_bytes=64, tag="grouped")
             grouped["a", r, c] = a_grouped
             copy(
-                out=a_grouped[:].rearrange("p (j q t) -> p q t j", j=PACK, t=PACK),
-                in_=a_raw[r, c][:].rearrange("p t (q j) -> p q t j", j=PACK),
+                out=a_grouped[:].rearrange("p (w i t) -> p w t i", i=4, t=PACK),
+                in_=a_raw[r, c][:].rearrange("p t (w i) -> p w t i", i=4),
             )
 
         def quantise_a(r, c, lanes=slice(0, PACK)):
@@ -236,7 +237,9 @@ def tile_gcnnodeclassifiernetwork_pb_kernel(
         transpose_h1(0)
         transpose_h1(1)
         quantise_h1(0)
-        nc.gpsimd.tensor_copy(out=d[:], in_=d_bf16[:].rearrange("p g j -> p (g j)"))
+        d_ps = psum_plain.tile([P, P], BF16, tag="plain")
+        nc.tensor.transpose(d_ps[:], d_rows[:], ident_bf16[:])
+        nc.scalar.copy(out=d[:], in_=d_ps[:, 0 : GROUPS * PACK])
         first_matmul(0)
         transpose_h1(2)
         regroup_a(0, 0, nc.vector.tensor_copy)

@@ -164,8 +164,8 @@ def tile_gcnnodeclassifiernetwork_pb_kernel(
             a_grouped = grouped_pool.tile([P, PACK * K_PASS], BF16, align_bytes=64, tag="grouped")
             grouped["a", r, c] = a_grouped
             copy(
-                out=a_grouped[:].rearrange("p (w i t) -> p w t i", i=4, t=PACK),
-                in_=a_raw[r, c][:].rearrange("p t (w i) -> p w t i", i=4),
+                out=a_grouped[:].rearrange("p (w i t) -> p w t i", i=8, t=PACK),
+                in_=a_raw[r, c][:].rearrange("p t (w i) -> p w t i", i=8),
             )
 
         def quantise_a(r, c, lanes=slice(0, PACK)):

@@ -36,15 +36,16 @@ def tile_gcnnodeclassifiernetwork_pb_kernel(
 
     with ExitStack() as ctx:
         keep = ctx.enter_context(tc.tile_pool(name="keep", bufs=1))
-        grouped_pool = ctx.enter_context(tc.tile_pool(name="grouped", bufs=6))
+        grouped_pool = ctx.enter_context(tc.tile_pool(name="grouped", bufs=6 + GROUPS))
         a_mx_pool = ctx.enter_context(tc.tile_pool(name="a_mx", bufs=2 * GROUPS))
-        total_pool = ctx.enter_context(tc.tile_pool(name="totals", bufs=PACK))
-        result_pool = ctx.enter_context(tc.tile_pool(name="results", bufs=2 * PACK))
+        total_pool = ctx.enter_context(tc.tile_pool(name="totals", bufs=GROUPS * PACK))
         psum_mx = ctx.enter_context(tc.psum_pool(name="psum_mx", bufs=4))
         psum_plain = ctx.enter_context(tc.psum_pool(name="psum_plain", bufs=4))
         ctx.enter_context(tc.manual_schedule())
 
-        h1_sb = [keep.tile([P, PACK, HID], BF16, name="h1_sb%d" % g) for g in range(GROUPS)]
+        h1_sb = []
+        for g in range(GROUPS):
+            h1_sb.append(grouped_pool.tile([P, PACK, HID], BF16, align_bytes=64, tag="grouped", name="h1_sb"))
         x_sb = [keep.tile([P, PACK, CLASSES], BF16, name="x_sb%d" % g) for g in range(GROUPS)]
         a_raw = {}
         for r in range(GROUPS):
@@ -66,6 +67,7 @@ def tile_gcnnodeclassifiernetwork_pb_kernel(
         for half in range(2):
             lanes = slice(2 * half, 2 * half + 2)
             nc.sync.dma_start(out=h1_sb[0][:, lanes, :], in_=h1_dram[0][:, lanes, :])
+        nc.sync.dma_start(out=h1_sb[1][:], in_=h1_dram[1])
         w2_plane = keep.tile([P, CLASSES], U8, align_bytes=64)
         nc.vector.memset(w2_plane[:].bitcast(I32), 0)
         for quadrant in range(4):
@@ -77,7 +79,6 @@ def tile_gcnnodeclassifiernetwork_pb_kernel(
         nc.sync.dma_start(
             out=w2_codes[:].bitcast(I32), in_=W2_words[0].rearrange("p n t -> p (n t)").bitcast(I32)
         )
-        nc.sync.dma_start(out=h1_sb[1][:], in_=h1_dram[1])
         d_rows = keep.tile([P, P], BF16)
         nc.vector.memset(d_rows[:], 0.0)
         nc.sync.dma_start(out=d_rows[0 : GROUPS * PACK, :], in_=deg_inv_sqrt.rearrange("(r p) -> r p", p=P))
@@ -209,7 +210,6 @@ def tile_gcnnodeclassifiernetwork_pb_kernel(
             )
 
         totals = {}
-        results = {}
         EVERY = slice(0, CLASSES)
 
         def finish_sum(r, j, classes=EVERY):
@@ -225,13 +225,9 @@ def tile_gcnnodeclassifiernetwork_pb_kernel(
             )
 
         def finish_sigmoid(r, j, classes=EVERY):
-            if (r, j) not in results:
-                results[r, j] = result_pool.tile([P, CLASSES], F32, name="result")
-            result = results[r, j]
-            nc.scalar.activation(
-                out=result[:, classes], in_=totals[r, j][:, classes], func=ACT.Sigmoid, scale=slope[:, 0:1]
-            )
-            nc.sync.dma_start(out=out_dram[r][:, j, classes], in_=result[:, classes])
+            result = totals[r, j][:, classes]
+            nc.scalar.activation(out=result, in_=result, func=ACT.Sigmoid, scale=slope[:, 0:1])
+            nc.sync.dma_start(out=out_dram[r][:, j, classes], in_=result)
 
         VECTOR_CHUNKS = LAST
         transpose_h1(0)

from contextlib import ExitStack

import concourse.mybir as mybir
from concourse.masks import make_identity

NODES = 2048
HID = 512
CLASSES = 512
FLOPS = 2 * NODES * HID * CLASSES + 2 * NODES * NODES * CLASSES

P = 128
PACK = 4
K_PASS = P * PACK
GROUPS = NODES // K_PASS
LAST = GROUPS - 1

BF16 = mybir.dt.bfloat16
F32 = mybir.dt.float32
I32 = mybir.dt.int32
U32 = mybir.dt.uint32
U8 = mybir.dt.uint8
FP8X4 = mybir.dt.float8_e4m3fn_x4
ACT = mybir.ActivationFunctionType
ALU = mybir.AluOpType


def tile_gcnnodeclassifiernetwork_pb_kernel(
    tc, A, deg_inv_sqrt, h1, W2_words, W2_scales, b2, x, sigmoid_param, out
):
    nc = tc.nc
    by_group = "(g j p) f -> g p j f"
    h1_dram = h1.rearrange(by_group, p=P, j=PACK)
    x_dram = x.rearrange(by_group, p=P, j=PACK)
    out_dram = out.rearrange(by_group, p=P, j=PACK)
    a_dram = A.rearrange(by_group, p=P, j=PACK)

    with ExitStack() as ctx:
        keep = ctx.enter_context(tc.tile_pool(name="keep", bufs=1))
        grouped_pool = ctx.enter_context(tc.tile_pool(name="grouped", bufs=6 + GROUPS))
        a_mx_pool = ctx.enter_context(tc.tile_pool(name="a_mx", bufs=2 * GROUPS))
        total_pool = ctx.enter_context(tc.tile_pool(name="totals", bufs=GROUPS * PACK))
        psum_mx = ctx.enter_context(tc.psum_pool(name="psum_mx", bufs=4))
        psum_plain = ctx.enter_context(tc.psum_pool(name="psum_plain", bufs=4))
        ctx.enter_context(tc.manual_schedule())

        h1_sb = []
        for g in range(GROUPS):
            h1_sb.append(grouped_pool.tile([P, PACK, HID], BF16, align_bytes=64, tag="grouped", name="h1_sb"))
        x_sb = [keep.tile([P, PACK, CLASSES], BF16, name="x_sb%d" % g) for g in range(GROUPS)]
        a_raw = {}
        for r in range(GROUPS):
            for c in range(GROUPS):
                a_raw[r, c] = keep.tile([P, PACK, K_PASS], BF16, name="a_raw%d_%d" % (r, c))
        h1t_codes = [keep.tile([P, K_PASS], U32, align_bytes=64, name="h1t_codes%d" % g) for g in range(GROUPS)]
        h1t_plane = [keep.tile([P, K_PASS], U8, align_bytes=64, name="h1t_plane%d" % g) for g in range(GROUPS)]
        m_codes = [keep.tile([P, CLASSES], U32, align_bytes=64, name="m_codes%d" % g) for g in range(GROUPS)]
        m_plane = [keep.tile([P, CLASSES], U8, align_bytes=64, name="m_plane%d" % g) for g in range(GROUPS)]
        own = [keep.tile([P, PACK, CLASSES], F32, name="own%d" % g) for g in range(GROUPS)]
        grouped = {}
        a_codes = {}
        a_plane = {}
        agg_ps = {}

        def load_a(r, c):
            nc.sync.dma_start(out=a_raw[r, c][:], in_=a_dram[c][:, :, K_PASS * r : K_PASS * (r + 1)])

        for half in range(2):
            lanes = slice(2 * half, 2 * half + 2)
            nc.sync.dma_start(out=h1_sb[0][:, lanes, :], in_=h1_dram[0][:, lanes, :])
        nc.sync.dma_start(out=h1_sb[1][:], in_=h1_dram[1])
        w2_plane = keep.tile([P, CLASSES], U8, align_bytes=64)
        nc.vector.memset(w2_plane[:].bitcast(I32), 0)
        for quadrant in range(4):
            nc.sync.dma_start(
                out=w2_plane[32 * quadrant : 32 * quadrant + 4, :].bitcast(I32),
                in_=W2_scales[0, 4 * quadrant : 4 * quadrant + 4, :].bitcast(I32),
            )
        w2_codes = keep.tile([P, PACK * CLASSES], U8, align_bytes=64)
        nc.sync.dma_start(
            out=w2_codes[:].bitcast(I32), in_=W2_words[0].rearrange("p n t -> p (n t)").bitcast(I32)
        )
        d_rows = keep.tile([P, P], BF16)
        nc.vector.memset(d_rows[:], 0.0)
        nc.sync.dma_start(out=d_rows[0 : GROUPS * PACK, :], in_=deg_inv_sqrt.rearrange("(r p) -> r p", p=P))
        load_a(0, 0)
        load_a(0, 1)
        nc.sync.dma_start(out=h1_sb[2][:], in_=h1_dram[2])
        load_a(0, 2)
        nc.sync.dma_start(out=h1_sb[3][:], in_=h1_dram[3])
        load_a(0, 3)
        b2_row = keep.tile([P, CLASSES], BF16)
        nc.vector.memset(b2_row[:], 0.0)
        nc.sync.dma_start(out=b2_row[0:1, :], in_=b2.unsqueeze(0))
        slope_bf16 = keep.tile([P, 1], BF16)
        nc.sync.dma_start(out=slope_bf16[:], in_=sigmoid_param.partition_broadcast(P))
        nc.sync.dma_start(out=x_sb[0][:], in_=x_dram[0])
        for r in range(1, GROUPS):
            for c in range(GROUPS):
                load_a(r, c)
            nc.sync.dma_start(out=x_sb[r][:], in_=x_dram[r])

        warm = keep.tile([P, 1], F32)
        nc.vector.memset(warm[:], 0.0)
        nc.scalar.activation(out=warm[:], in_=warm[:], func=ACT.Sigmoid)

        ident_f32 = keep.tile([P, P], F32)
        make_identity(nc, ident_f32[:])
        ident_bf16 = keep.tile([P, P], BF16)
        make_identity(nc, ident_bf16[:])
        ones = keep.tile([P, P], BF16)
        nc.vector.memset(ones[:], 1.0)

        d = keep.tile([P, GROUPS * PACK], F32)
        slope = keep.tile([P, 1], F32)

        def d_of(g, j):
            return d[:, PACK * g + j : PACK * g + j + 1]

        def transpose_h1(g):
            h1t = grouped_pool.tile([P, PACK * K_PASS], BF16, align_bytes=64, tag="grouped")
            grouped["h1", g] = h1t
            h1t_words = h1t[:].bitcast(F32).rearrange("q (j n u) -> q j n u", j=PACK, u=2)
            for half in range(2):
                bank = psum_plain.tile([P, 2, 2, P], F32, tag="plain")
                for lane in range(2):
                    words = h1_sb[g][:, 2 * half + lane, :].bitcast(F32)
                    for u in range(2):
                        nc.tensor.transpose(bank[:, lane, u, :], words[:, u : HID // 2 : 2], ident_f32[:])
                nc.scalar.copy(
                    out=h1t_words[:, 2 * half : 2 * half + 2], in_=bank[:].rearrange("q j u n -> q j n u")
                )

        def quantise_h1(g):
            nc.vector.quantize_mx(
                out=h1t_codes[g][:].bitcast(FP8X4), scales=h1t_plane[g][:], in_=grouped["h1", g][:]
            )

        def first_matmul(g):
            for j in range(PACK):
                lane_cols = slice(P * j, P * (j + 1))
                g_ps = psum_mx.tile([P, CLASSES], F32, tag="mx")
                nc.tensor.matmul_mx(
                    out=g_ps[:],
                    lhsT=h1t_codes[g][:, lane_cols].bitcast(FP8X4),
                    lhsT_scale=h1t_plane[g][:, lane_cols],
                    rhs=w2_codes[:].bitcast(FP8X4),
                    rhs_scale=w2_plane[:],
                    start=True,
                    stop=True,
                )
                nc.scalar.activation(out=own[g][:, j, :], in_=g_ps[:], func=ACT.Copy, scale=d_of(g, j))

        def regroup_m(g):
            m_grouped = grouped_pool.tile([P, PACK * CLASSES], BF16, align_bytes=64, tag="grouped")
            grouped["m", g] = m_grouped
            nc.vector.tensor_copy(
                out=m_grouped[:].rearrange("p (n i j) -> p n j i", i=4, j=PACK),
                in_=own[g][:].rearrange("p j (n i) -> p n j i", i=4),
            )

        def quantise_m(g):
            nc.vector.quantize_mx(out=m_codes[g][:].bitcast(FP8X4), scales=m_plane[g][:], in_=grouped["m", g][:])

        def regroup_a(r, c, copy):
            a_grouped = grouped_pool.tile([P, PACK * K_PASS], BF16, align_bytes=64, tag="grouped")
            grouped["a", r, c] = a_grouped
            copy(
                out=a_grouped[:].rearrange("p (w i t) -> p w t i", i=8, t=PACK),
                in_=a_raw[r, c][:].rearrange("p t (w i) -> p w t i", i=8),
            )

        def quantise_a(r, c, lanes=slice(0, PACK)):
            if (r, c) not in a_codes:
                a_codes[r, c] = a_mx_pool.tile([P, K_PASS], U32, align_bytes=64, tag="a_codes", name="a_codes")
                a_plane[r, c] = a_mx_pool.tile([P, K_PASS], U8, align_bytes=64, tag="a_plane", name="a_plane")
            cols = slice(P * lanes.start, P * lanes.stop)
            nc.vector.quantize_mx(
                out=a_codes[r, c][:, cols].bitcast(FP8X4),
                scales=a_plane[r, c][:, cols],
                in_=grouped["a", r, c][:, PACK * cols.start : PACK * cols.stop],
            )

        def add_skip_and_bias(r, lanes=range(PACK)):
            for j in lanes:
                skip_ps = psum_plain.tile([P, CLASSES], F32, tag="plain")
                nc.tensor.matmul(skip_ps[:], lhsT=ident_bf16[:], rhs=x_sb[r][:, j, :], start=True, stop=False)
                nc.tensor.matmul(skip_ps[:], lhsT=ones[:], rhs=b2_row[:], start=False, stop=True)
                nc.vector.scalar_tensor_tensor(
                    out=own[r][:, j, :],
                    in0=own[r][:, j, :],
                    scalar=d_of(r, j),
                    in1=skip_ps[:],
                    op0=ALU.mult,
                    op1=ALU.add,
                )

        def second_matmul_pass(r, j, c):
            if c == 0:
                bank_pool, bank_tag = (psum_plain, "plain") if r == LAST else (psum_mx, "mx")
                agg_ps[r, j] = bank_pool.tile([P, CLASSES], F32, tag=bank_tag, name="agg_ps")
            lane_cols = slice(P * j, P * (j + 1))
            nc.tensor.matmul_mx(
                out=agg_ps[r, j][:],
                lhsT=a_codes[r, c][:, lane_cols].bitcast(FP8X4),
                lhsT_scale=a_plane[r, c][:, lane_cols],
                rhs=m_codes[c][:].bitcast(FP8X4),
                rhs_scale=m_plane[c][:],
                start=(c == 0),
                stop=(c == LAST),
            )

        totals = {}
        EVERY = slice(0, CLASSES)

        def finish_sum(r, j, classes=EVERY):
            if (r, j) not in totals:
                totals[r, j] = total_pool.tile([P, CLASSES], F32, name="total")
            nc.vector.scalar_tensor_tensor(
                out=totals[r, j][:, classes],
                in0=agg_ps[r, j][:, classes],
                scalar=d_of(r, j),
                in1=own[r][:, j, classes],
                op0=ALU.mult,
                op1=ALU.add,
            )

        def finish_sigmoid(r, j, classes=EVERY):
            result = totals[r, j][:, classes]
            nc.scalar.activation(out=result, in_=result, func=ACT.Sigmoid, scale=slope[:, 0:1])
            nc.sync.dma_start(out=out_dram[r][:, j, classes], in_=result)

        VECTOR_CHUNKS = LAST
        transpose_h1(0)
        transpose_h1(1)
        quantise_h1(0)
        d_ps = psum_plain.tile([P, P], BF16, tag="plain")
        nc.tensor.transpose(d_ps[:], d_rows[:], ident_bf16[:])
        nc.scalar.copy(out=d[:], in_=d_ps[:, 0 : GROUPS * PACK])
        first_matmul(0)
        transpose_h1(2)
        regroup_a(0, 0, nc.vector.tensor_copy)
        quantise_h1(1)
        first_matmul(1)
        transpose_h1(3)
        for k in range(GROUPS):
            if k < VECTOR_CHUNKS:
                quantise_a(0, k)
            if k == 0 and k + 1 < VECTOR_CHUNKS:
                regroup_a(0, k + 1, nc.vector.tensor_copy)
            regroup_m(k)
            if k + 2 < GROUPS:
                quantise_h1(k + 2)
                first_matmul(k + 2)
            else:
                add_skip_and_bias(0, [k - 2])
            if k > 0 and k + 1 < VECTOR_CHUNKS:
                regroup_a(0, k + 1, nc.vector.tensor_copy)
            quantise_m(k)
        nc.gpsimd.tensor_copy(out=slope[:], in_=slope_bf16[:])
        regroup_a(0, LAST, nc.scalar.copy)
        regroup_a(1, 0, nc.scalar.copy)
        add_skip_and_bias(0, [2, 3])
        quantise_a(0, LAST)

        for r in range(GROUPS):
            if r + 1 < GROUPS:
                regroup_a(r + 1, 1, nc.scalar.copy)
                regroup_a(r + 1, 2, nc.scalar.copy)
            if r + 2 < GROUPS:
                regroup_a(r + 2, 0, nc.scalar.copy)
            if r + 1 < GROUPS:
                add_skip_and_bias(r + 1)
                regroup_a(r + 1, LAST, nc.vector.tensor_copy)
            if r < LAST:
                for j in range(PACK):
                    for c in range(GROUPS):
                        second_matmul_pass(r, j, c)
            for j in range(PACK):
                if (r + 1, j) == (LAST, LAST):
                    quantise_a(LAST, LAST, slice(0, 2))
                halves = [slice(0, CLASSES // 2), slice(CLASSES // 2, CLASSES)] if (r, j) == (LAST, LAST) else [EVERY]
                for classes in halves:
                    finish_sum(r, j, classes)
                    finish_sigmoid(r, j, classes)
                if (r + 1, j) == (LAST, LAST):
                    quantise_a(LAST, LAST, slice(2, PACK))
                elif r + 1 < GROUPS:
                    quantise_a(r + 1, j)
                if r + 1 == LAST:
                    if j < 2:
                        for lane in range(PACK):
                            second_matmul_pass(LAST, lane, j)
                    if j == LAST:
                        for lanes in ((0, 1), (2, 3)):
                            for c in (2, 3):
                                for lane in lanes:
                                    second_matmul_pass(LAST, lane, c)
